import numpy as np
import ml_dtypes


def mxq(x, axis, fmt="e4m3"):
    dtype, down = {"e4m3": (ml_dtypes.float8_e4m3fn, 7), "e5m2": (ml_dtypes.float8_e5m2, 14)}[fmt]
    v = np.moveaxis(np.asarray(x, np.float32).astype(ml_dtypes.bfloat16).astype(np.float64), axis, -1)
    blocks = v.reshape(v.shape[:-1] + (-1, 32))
    amax = np.abs(blocks).max(-1, keepdims=True)
    byte = np.maximum(np.where(amax > 0, np.frexp(amax)[1] - 1 + 127, 0) - down, 1)
    scale = np.exp2(byte - 127.0)
    codes = (blocks / scale).astype(np.float32).astype(dtype).astype(np.float64)
    return np.moveaxis((codes * scale).reshape(v.shape), -1, axis)


WIDE = False


def mx_kscale(k):
    if not WIDE:
        return np.ones(k)
    levels = np.array([30, -30])
    if k % 512:
        return np.exp2(np.random.permutation(np.resize(levels, k // 32))).repeat(32)
    a = np.empty((k // 512, 16))
    for p in range(k // 512):
        a[p, :8] = np.random.permutation(np.resize(levels, 8))
        for g in range(8):
            far = levels[np.abs(levels - a[p, g]) >= 10]
            a[p, g + 8] = far[np.random.randint(len(far))]
    return np.exp2(a.ravel()).repeat(32)


BF16 = ml_dtypes.bfloat16


def bf(x):
    return np.asarray(x, np.float32).astype(BF16)


def f64(x):
    return np.asarray(x).astype(np.float64)


B, D_IN, D_OUT = 1024, 1024, 1024


def sigmoid(v):
    return 1.0 / (1.0 + np.exp(-v))


def setup_inputs():
    s, t = mx_kscale(D_IN), mx_kscale(D_OUT)

    def wx():
        return bf(np.random.standard_normal((D_IN, D_OUT)) / np.sqrt(D_IN) / s[:, None])

    def wh():
        return bf(np.random.standard_normal((D_OUT, D_OUT)) / np.sqrt(D_OUT) / t[:, None])

    return {"x": bf(np.random.standard_normal((B, D_IN)) * s),
            "hist": bf(np.random.standard_normal((B, D_OUT)) * t),
            "ig": bf(np.random.standard_normal((B, D_OUT)) * 0.4),
            "carousel": bf(np.random.uniform(1.25, 1.75, 1)),
            "Wfx": wx(), "Wfh": wh(), "b_f": bf(np.random.standard_normal(D_OUT) * 0.3),
            "Wox": wx(), "Woh": wh(), "b_o": bf(np.random.standard_normal(D_OUT) * 0.3)}


def reference(x, hist, ig, carousel, Wfx, Wfh, b_f, Wox, Woh, b_o):
    xq = mxq(f64(x), 1, "e5m2")
    hq = mxq(f64(hist), 1, "e5m2")
    f = sigmoid((xq @ mxq(f64(Wfx), 0, "e5m2")) + (hq @ mxq(f64(Wfh), 0, "e5m2")) + f64(b_f))
    o = sigmoid((xq @ mxq(f64(Wox), 0, "e5m2")) + (hq @ mxq(f64(Woh), 0, "e5m2")) + f64(b_o))
    c = f * f64(carousel) + f64(ig)
    h = o * c
    return (h, c)

@@ -1,0 +1,271 @@
+from contextlib import ExitStack
+
+import concourse.mybir as mybir
+from concourse.masks import make_identity
+
+B, K, N = 1024, 1024, 1024
+FLOPS = 4 * 2 * B * K * N
+
+F32 = mybir.dt.float32
+BF16 = mybir.dt.bfloat16
+U32 = mybir.dt.uint32
+U8 = mybir.dt.uint8
+E5M2X4 = mybir.dt.float8_e5m2_x4
+ADD = mybir.AluOpType.add
+MULT = mybir.AluOpType.mult
+SIGMOID = mybir.ActivationFunctionType.Sigmoid
+
+P = 128
+PACK = 4
+K_PASS = P * PACK
+QW = 256
+BANK = 512
+
+
+def tile_lstmmirrored_pb_kernel(tc, x, hist, ig, carousel, Wfx, Wfh, b_f, Wox, Woh, b_o, out_0, out_1):
+    nc = tc.nc
+    acts = (x, hist)
+    weights = ((Wfx, Wox), (Wfh, Woh))
+
+    def rows_view(t):
+        return t.rearrange("(H p r) n -> H p r n", H=2, r=4)
+
+    with ExitStack() as ctx:
+        keep = ctx.enter_context(tc.tile_pool(name="keep", bufs=1))
+        stream = ctx.enter_context(tc.tile_pool(name="stream", bufs=1))
+        psum = ctx.enter_context(tc.psum_pool(name="psum", bufs=8))
+        ctx.enter_context(tc.manual_schedule(engines={mybir.EngineType.SP}))
+
+        ident = keep.tile([P, P], F32, name="ident")
+        ones = keep.tile([P, P], BF16, name="ones")
+        bias_row = stream.tile([P, 2 * N], BF16, name="bias_row", tag="gates", bufs=4)
+        bias = keep.tile([P, 2, N], BF16, name="bias")
+        gain = keep.tile([P, 1], BF16, name="gain")
+        make_identity(nc, ident[:])
+        nc.vector.memset(bias_row[:].bitcast(U32), 0)
+        nc.vector.memset(ones[:], 1.0)
+
+        w_raw, a_raw, ig_sb = {}, {}, {}
+        w_grouped, a_grouped, w_q, a_q = {}, {}, {}, {}
+        acc, gates, c_out, h_out, a_banks = {}, {}, {}, {}, {}
+
+        def raw_tile(shape, name):
+            return stream.tile(shape, BF16, name=name, tag="raw", bufs=20)
+
+        def load_w(kp, q0, n_q):
+            s, g = divmod(kp, 2)
+            if n_q == 1:
+                both = raw_tile([P, 2, PACK, QW], "w%d%d" % (kp, q0))
+            for gate in range(2):
+                t = both[:, gate, :, :] if n_q == 1 else raw_tile([P, PACK, BANK], "w%d%d%d" % (kp, q0, gate))[:]
+                src = weights[s][gate][g * K_PASS : (g + 1) * K_PASS, q0 * QW : (q0 + n_q) * QW]
+                nc.sync.dma_start(out=t, in_=src.rearrange("(p j) n -> p j n", j=PACK))
+                for d in range(n_q):
+                    w_raw[kp, q0 + d, gate] = t[:, :, d * QW : (d + 1) * QW]
+
+        def load_a(s, H, rp):
+            t = raw_tile([P, 2, K], "a%d%d%d" % (s, H, rp))
+            nc.sync.dma_start(out=t[:], in_=rows_view(acts[s])[H, :, 2 * rp : 2 * rp + 2, :])
+            a_raw[s, H, rp] = t
+
+        def load_ig(H, half):
+            t = keep.tile([P, 4, BANK], BF16, name="ig%d%d" % (H, half))
+            nc.sync.dma_start(out=t[:], in_=rows_view(ig)[H, :, :, half * BANK : (half + 1) * BANK])
+            ig_sb[H, half] = t
+
+        def load_consts():
+            for gate, b in enumerate((b_f, b_o)):
+                nc.sync.dma_start(out=bias_row[0:1, gate * N : (gate + 1) * N], in_=b.rearrange("(o n) -> o n", o=1))
+            nc.sync.dma_start(out=gain[:], in_=carousel.partition_broadcast(P))
+
+        def spread_bias():
+            for gate in range(2):
+                bank = psum.tile([P, N], BF16, name="bias_bank%d" % gate, tag="bank")
+                for c0 in range(0, N, BANK):
+                    nc.tensor.matmul(bank[:, c0 : c0 + BANK], ones[:], bias_row[:, gate * N + c0 : gate * N + c0 + BANK], start=True, stop=True)
+                nc.scalar.copy(out=bias[:, gate, :], in_=bank[:])
+
+        def grouped_tile(name):
+            return stream.tile([P, PACK * BANK], BF16, name=name, tag="grouped", bufs=5, align_bytes=64)
+
+        def interleave_w(q, kp, gate, on_vector):
+            if (q, kp) not in w_grouped:
+                w_grouped[q, kp] = grouped_tile("wg%d%d" % (q, kp))
+            dst = w_grouped[q, kp][:, gate * PACK * QW : (gate + 1) * PACK * QW].rearrange("p (c i t) -> p c t i", i=4, t=PACK)
+            src = w_raw[kp, q, gate].rearrange("p t (c i) -> p c t i", i=4)
+            if on_vector:
+                nc.vector.tensor_copy(out=dst, in_=src)
+            else:
+                nc.scalar.copy(out=dst, in_=src)
+
+        def quantize(grouped, name):
+            codes = keep.tile([P, BANK], U32, name=name + "_codes", align_bytes=64)
+            scales = keep.tile([P, BANK], U8, name=name + "_scales", align_bytes=64)
+            nc.vector.quantize_mx(out=codes[:].bitcast(E5M2X4), scales=scales[:], in_=grouped[:])
+            return codes, scales
+
+        def quantize_w(q, kp):
+            w_q[q, kp] = quantize(w_grouped[q, kp], "wq%d%d" % (q, kp))
+
+        def transpose_a(s, H, rp):
+            banks = a_banks[s, H, rp] = []
+            for r in range(2):
+                bank = psum.tile([P, 2, 2, P], F32, name="tr%d%d%d%d" % (s, H, rp, r), tag="bank")
+                words = a_raw[s, H, rp][:, r, :].bitcast(F32)
+                for g in range(2):
+                    for u in range(2):
+                        nc.tensor.transpose(bank[:, g, u, :], words[:, 256 * g + u : 256 * (g + 1) : 2], ident[:])
+                banks.append(bank)
+
+        def copy_a(s, H, rp):
+            a_grouped[s, H, rp] = grouped_tile("ag%d%d%d" % (s, H, rp))
+            banks = a_banks[s, H, rp]
+            for r in range(2):
+                dst = a_grouped[s, H, rp][:].bitcast(F32)[:, r * BANK : (r + 1) * BANK]
+                nc.scalar.copy(out=dst.rearrange("p (g b u) -> p g b u", g=2, u=2), in_=banks[r][:].rearrange("p g u b -> p g b u"))
+
+        def quantize_a(s, H, rp):
+            a_q[s, H, rp] = quantize(a_grouped[s, H, rp], "aq%d%d%d" % (s, H, rp))
+
+        def mx_pass(step, r, kp):
+            q, H, rp = step
+            s, g = divmod(kp, 2)
+            if kp == 0:
+                acc[step, r] = psum.tile([P, BANK], F32, name="acc%d%d%d%d" % (q, H, rp, r), tag="bank")
+            a_codes, a_scales = a_q[s, H, rp]
+            w_codes, w_scales = w_q[q, kp]
+            cols = slice((2 * r + g) * P, (2 * r + g + 1) * P)
+            nc.tensor.matmul_mx(
+                out=acc[step, r][:],
+                lhsT=a_codes[:, cols].bitcast(E5M2X4),
+                lhsT_scale=a_scales[:, cols],
+                rhs=w_codes[:].bitcast(E5M2X4),
+                rhs_scale=w_scales[:],
+                start=(kp == 0),
+                stop=(kp == 3),
+            )
+
+        def multiply(step):
+            for r in range(2):
+                for kp in range(4):
+                    mx_pass(step, r, kp)
+
+        def add_bias(step, r):
+            q = step[0]
+            if r == 0:
+                gates[step] = stream.tile([P, 2, 2, QW], F32, name="gates%d%d%d" % step, tag="gates", bufs=4)
+            nc.vector.tensor_tensor(
+                out=gates[step][:, r, :, :],
+                in0=acc[step, r][:].rearrange("p (e n) -> p e n", e=2),
+                in1=bias[:, :, q * QW : (q + 1) * QW],
+                op=ADD,
+            )
+
+        def sigmoid(step):
+            flat = gates[step][:].rearrange("p r e n -> p (r e n)")
+            nc.scalar.activation(out=flat, in_=flat, func=SIGMOID)
+
+        def cell(step):
+            q, H, rp = step
+            if rp == 0:
+                c_out[q, H] = stream.tile([P, 4, QW], F32, name="c%d%d" % (q, H), tag="out", bufs=10)
+                h_out[q, H] = stream.tile([P, 4, QW], F32, name="h%d%d" % (q, H), tag="out", bufs=10)
+            c0 = (q % 2) * QW
+            nc.vector.scalar_tensor_tensor(
+                out=c_out[q, H][:, 2 * rp : 2 * rp + 2, :],
+                in0=gates[step][:, :, 0, :],
+                scalar=gain[:],
+                in1=ig_sb[H, q // 2][:, 2 * rp : 2 * rp + 2, c0 : c0 + QW],
+                op0=MULT,
+                op1=ADD,
+            )
+
+        def hidden(step, engine):
+            q, H, rp = step
+            rows = slice(2 * rp, 2 * rp + 2)
+            engine.tensor_tensor(out=h_out[q, H][:, rows, :], in0=gates[step][:, :, 1, :], in1=c_out[q, H][:, rows, :], op=MULT)
+
+        def store(q, H, rows):
+            for dst, src in ((out_1, c_out), (out_0, h_out)):
+                nc.sync.dma_start(out=rows_view(dst)[H, :, rows, q * QW : (q + 1) * QW], in_=src[q, H][:, rows, :])
+
+
+        V, S = True, False
+        for item in [("w",0,0,2),("a",0,0),"c",("w",1,0,2),("a",1,0),("w",2,0,2),("a",0,1),("w",3,0,2),("a",1,1),("g",0,0),("a",0,2),("a",1,2),("w",0,2,2),("a",0,3),("a",1,3),("g",1,0),("w",1,2,2),("w",2,2,2),("w",3,2,2),("g",0,1),("g",1,1)]:
+            if item == "c":
+                load_consts()
+            elif item[0] == "w":
+                load_w(*item[1:])
+            elif item[0] == "a":
+                load_a(item[1], item[2] // 2, item[2] % 2)
+            else:
+                load_ig(*item[1:])
+        onv = [["VV","VV","VV","VS"],["SS","SS","SV","SV"],["VS","VS","SS","SS"],["SS","VS","SS","VS"]]
+        def prep_w(q, kp):
+            interleave_w(q, kp, 0, onv[q][kp][0] == "V")
+            interleave_w(q, kp, 1, onv[q][kp][1] == "V")
+            return (quantize_w, q, kp)
+        def prep_a(s, p):
+            transpose_a(s, p // 2, p % 2)
+            copy_a(s, p // 2, p % 2)
+            return (quantize_a, s, p // 2, p % 2)
+        pending = []
+        def prep(item):
+            new = prep_w(*item[1:]) if item[0] == "w" else prep_a(*item[1:])
+            flush()
+            pending.append(new)
+        def flush():
+            for f, *a in pending:
+                f(*a)
+            pending.clear()
+        steps = [(q, p // 2, p % 2) for q, p in [(0,0),(1,0),(0,1),(1,1),(0,2),(1,2),(0,3),(1,3),(2,0),(2,1),(2,2),(2,3),(3,0),(3,1),(3,2),(3,3)]]
+        n_steps = len(steps)
+        done = set()
+        def early(step, kps):
+            flush()
+            for kp in kps:
+                for r in range(2):
+                    mx_pass(step, r, kp)
+                    done.add((step, r, kp))
+        def mult(step):
+            flush()
+            for r in range(2):
+                for kp in range(4):
+                    if (step, r, kp) not in done:
+                        mx_pass(step, r, kp)
+        for item in [("w",0,0),("a",0,0),("w",1,0),"b",("w",0,1),("w",1,1),("e",0,[0,1]),("a",1,0),("e",1,[0,1]),("w",0,2),("a",0,1),("w",1,2),("e",0,[2]),("e",1,[2]),("w",0,3),("w",1,3)]:
+            if item == "b":
+                spread_bias()
+            elif item[0] == "e":
+                early(steps[item[1]], item[2])
+            else:
+                prep(item)
+        extras = {0:[("a",1,1)],1:[("a",0,2)],2:[("a",1,2),("w",2,0)],3:[("a",0,3)],4:[("a",1,3),("w",2,1)],5:[("w",2,2)],6:[("w",2,3)],7:[("w",3,0)],8:[("w",3,1)],9:[("w",3,2)],10:[("w",3,3)]}
+        AH = 1
+        for i in range(AH):
+            mult(steps[i])
+        stores = []
+        seen = set()
+        LAG = 2
+        for i in range(n_steps + LAG):
+            pool = False
+            if i >= LAG:
+                cell(steps[i - LAG])
+                if pool:
+                    hidden(steps[i - LAG], nc.gpsimd)
+            if i < n_steps:
+                add_bias(steps[i], 0)
+                add_bias(steps[i], 1)
+                sigmoid(steps[i])
+            if i >= LAG:
+                if not pool:
+                    hidden(steps[i - LAG], nc.vector)
+                q, H, rp = steps[i - LAG]
+                if i - LAG >= n_steps - 4:
+                    store(q, H, slice(2 * rp, 2 * rp + 2))
+                elif rp == 1:
+                    store(q, H, slice(0, 4))
+            for item in extras.get(i, []):
+                prep(item)
+            if i + AH < n_steps:
+                mult(steps[i + AH])

@@ -25,10 +25,10 @@ BANK = 512
 def tile_lstmmirrored_pb_kernel(tc, x, hist, ig, carousel, Wfx, Wfh, b_f, Wox, Woh, b_o, out_0, out_1):
     nc = tc.nc
     acts = (x, hist)
-    weights = ((Wfx, Wox), (Wfh, Woh))
+    weights = ((Wfx, Wfh), (Wox, Woh))
 
-    def rows_view(t):
-        return t.rearrange("(H p r) n -> H p r n", H=2, r=4)
+    def pair_rows(t, pair):
+        return t.rearrange("(m p r) n -> m p r n", m=4, r=2)[pair]
 
     with ExitStack() as ctx:
         keep = ctx.enter_context(tc.tile_pool(name="keep", bufs=1))
@@ -40,6 +40,7 @@ def tile_lstmmirrored_pb_kernel(tc, x, hist, ig, carousel, Wfx, Wfh, b_f, Wox, W
         ones = keep.tile([P, P], BF16, name="ones")
         bias_row = stream.tile([P, 2 * N], BF16, name="bias_row", tag="gates", bufs=4)
         bias = keep.tile([P, 2, N], BF16, name="bias")
+        bias_col = keep.tile([P, 2 * N // P], F32, name="bias_col")
         gain = keep.tile([P, 1], BF16, name="gain")
         make_identity(nc, ident[:])
         nc.vector.memset(bias_row[:].bitcast(U32), 0)
@@ -47,31 +48,32 @@ def tile_lstmmirrored_pb_kernel(tc, x, hist, ig, carousel, Wfx, Wfh, b_f, Wox, W
 
         w_raw, a_raw, ig_sb = {}, {}, {}
         w_grouped, a_grouped, w_q, a_q = {}, {}, {}, {}
-        acc, gates, c_out, h_out, a_banks = {}, {}, {}, {}, {}
+        acc, gates, c_out, h_out, a_banks, back = {}, {}, {}, {}, {}, {}
 
-        def raw_tile(shape, name):
-            return stream.tile(shape, BF16, name=name, tag="raw", bufs=20)
-
-        def load_w(kp, q0, n_q):
+        def load_w(gate, kp, splits=1, halves=(0, 1)):
             s, g = divmod(kp, 2)
-            if n_q == 1:
-                both = raw_tile([P, 2, PACK, QW], "w%d%d" % (kp, q0))
-            for gate in range(2):
-                t = both[:, gate, :, :] if n_q == 1 else raw_tile([P, PACK, BANK], "w%d%d%d" % (kp, q0, gate))[:]
-                src = weights[s][gate][g * K_PASS : (g + 1) * K_PASS, q0 * QW : (q0 + n_q) * QW]
-                nc.sync.dma_start(out=t, in_=src.rearrange("(p j) n -> p j n", j=PACK))
-                for d in range(n_q):
-                    w_raw[kp, q0 + d, gate] = t[:, :, d * QW : (d + 1) * QW]
+            src = weights[gate][s][g * K_PASS : (g + 1) * K_PASS, :].rearrange("(p j) n -> p j n", j=PACK)
+            if splits == 1:
+                t = stream.tile([P, PACK, N], BF16, name="w%d%d" % (gate, kp), tag="w_raw", bufs=5)
+                nc.sync.dma_start(out=t[:], in_=src)
+            for half in halves:
+                cols = slice(half * BANK, (half + 1) * BANK)
+                if splits == 2:
+                    t = stream.tile([P, PACK, BANK], BF16, name="w%d%d%d" % (gate, kp, half), tag="a_raw", bufs=7)
+                    nc.sync.dma_start(out=t[:], in_=src[:, :, cols])
+                    w_raw[2 * gate + half, kp] = t[:]
+                else:
+                    w_raw[2 * gate + half, kp] = t[:, :, cols]
 
-        def load_a(s, H, rp):
-            t = raw_tile([P, 2, K], "a%d%d%d" % (s, H, rp))
-            nc.sync.dma_start(out=t[:], in_=rows_view(acts[s])[H, :, 2 * rp : 2 * rp + 2, :])
-            a_raw[s, H, rp] = t
+        def load_a(s, pair):
+            t = stream.tile([P, 2, K], BF16, name="a%d%d" % (s, pair), tag="a_raw", bufs=7)
+            nc.sync.dma_start(out=t[:], in_=pair_rows(acts[s], pair))
+            a_raw[s, pair] = t
 
-        def load_ig(H, half):
-            t = keep.tile([P, 4, BANK], BF16, name="ig%d%d" % (H, half))
-            nc.sync.dma_start(out=t[:], in_=rows_view(ig)[H, :, :, half * BANK : (half + 1) * BANK])
-            ig_sb[H, half] = t
+        def load_ig(pair):
+            t = keep.tile([P, 2, N], BF16, name="ig%d" % pair)
+            nc.sync.dma_start(out=t[:], in_=pair_rows(ig, pair))
+            ig_sb[pair] = t
 
         def load_consts():
             for gate, b in enumerate((b_f, b_o)):
@@ -85,14 +87,20 @@ def tile_lstmmirrored_pb_kernel(tc, x, hist, ig, carousel, Wfx, Wfh, b_f, Wox, W
                     nc.tensor.matmul(bank[:, c0 : c0 + BANK], ones[:], bias_row[:, gate * N + c0 : gate * N + c0 + BANK], start=True, stop=True)
                 nc.scalar.copy(out=bias[:, gate, :], in_=bank[:])
 
+        def turn_bias():
+            bank = psum.tile([P, 2 * N // P], F32, name="bias_col_bank", tag="bank")
+            for blk in range(2 * N // P):
+                nc.tensor.matmul(bank[:, blk : blk + 1], bias_row[:, blk * P : (blk + 1) * P], ones[:, 0:1], start=True, stop=True)
+            nc.scalar.copy(out=bias_col[:], in_=bank[:])
+
         def grouped_tile(name):
             return stream.tile([P, PACK * BANK], BF16, name=name, tag="grouped", bufs=5, align_bytes=64)
 
-        def interleave_w(q, kp, gate, on_vector):
-            if (q, kp) not in w_grouped:
-                w_grouped[q, kp] = grouped_tile("wg%d%d" % (q, kp))
-            dst = w_grouped[q, kp][:, gate * PACK * QW : (gate + 1) * PACK * QW].rearrange("p (c i t) -> p c t i", i=4, t=PACK)
-            src = w_raw[kp, q, gate].rearrange("p t (c i) -> p c t i", i=4)
+        def piece(grp, kp, part, on_vector):
+            if (grp, kp) not in w_grouped:
+                w_grouped[grp, kp] = grouped_tile("wg%d%d" % (grp, kp))
+            dst = w_grouped[grp, kp][:, part * PACK * QW : (part + 1) * PACK * QW].rearrange("p (c i t) -> p c t i", i=4, t=PACK)
+            src = w_raw[grp, kp][:, :, part * QW : (part + 1) * QW].rearrange("p t (c i) -> p c t i", i=4)
             if on_vector:
                 nc.vector.tensor_copy(out=dst, in_=src)
             else:
@@ -104,37 +112,34 @@ def tile_lstmmirrored_pb_kernel(tc, x, hist, ig, carousel, Wfx, Wfh, b_f, Wox, W
             nc.vector.quantize_mx(out=codes[:].bitcast(E5M2X4), scales=scales[:], in_=grouped[:])
             return codes, scales
 
-        def quantize_w(q, kp):
-            w_q[q, kp] = quantize(w_grouped[q, kp], "wq%d%d" % (q, kp))
+        def quantize_w(grp, kp):
+            w_q[grp, kp] = quantize(w_grouped[grp, kp], "wq%d%d" % (grp, kp))
 
-        def transpose_a(s, H, rp):
-            banks = a_banks[s, H, rp] = []
+        def turn_a(s, pair):
+            banks = []
             for r in range(2):
-                bank = psum.tile([P, 2, 2, P], F32, name="tr%d%d%d%d" % (s, H, rp, r), tag="bank")
-                words = a_raw[s, H, rp][:, r, :].bitcast(F32)
+                bank = psum.tile([P, 2, 2, P], F32, name="tr%d%d%d" % (s, pair, r), tag="bank")
+                words = a_raw[s, pair][:, r, :].bitcast(F32)
                 for g in range(2):
                     for u in range(2):
                         nc.tensor.transpose(bank[:, g, u, :], words[:, 256 * g + u : 256 * (g + 1) : 2], ident[:])
                 banks.append(bank)
-
-        def copy_a(s, H, rp):
-            a_grouped[s, H, rp] = grouped_tile("ag%d%d%d" % (s, H, rp))
-            banks = a_banks[s, H, rp]
+            a_grouped[s, pair] = grouped_tile("ag%d%d" % (s, pair))
+            dst = a_grouped[s, pair][:].bitcast(F32).rearrange("p (g r b u) -> p r g b u", g=2, r=2, u=2)
             for r in range(2):
-                dst = a_grouped[s, H, rp][:].bitcast(F32)[:, r * BANK : (r + 1) * BANK]
-                nc.scalar.copy(out=dst.rearrange("p (g b u) -> p g b u", g=2, u=2), in_=banks[r][:].rearrange("p g u b -> p g b u"))
+                nc.scalar.copy(out=dst[:, r, :, :, :], in_=banks[r][:].rearrange("p g u b -> p g b u"))
 
-        def quantize_a(s, H, rp):
-            a_q[s, H, rp] = quantize(a_grouped[s, H, rp], "aq%d%d%d" % (s, H, rp))
+        def quant_a(s, pair):
+            a_q[s, pair] = quantize(a_grouped[s, pair], "aq%d%d" % (s, pair))
 
         def mx_pass(step, r, kp):
-            q, H, rp = step
+            grp, pair = step
             s, g = divmod(kp, 2)
             if kp == 0:
-                acc[step, r] = psum.tile([P, BANK], F32, name="acc%d%d%d%d" % (q, H, rp, r), tag="bank")
-            a_codes, a_scales = a_q[s, H, rp]
-            w_codes, w_scales = w_q[q, kp]
-            cols = slice((2 * r + g) * P, (2 * r + g + 1) * P)
+                acc[step, r] = psum.tile([P, BANK], F32, name="acc%d%d%d" % (grp, pair, r), tag="bank")
+            a_codes, a_scales = a_q[s, pair]
+            w_codes, w_scales = w_q[grp, kp]
+            cols = slice((2 * g + r) * P, (2 * g + r + 1) * P)
             nc.tensor.matmul_mx(
                 out=acc[step, r][:],
                 lhsT=a_codes[:, cols].bitcast(E5M2X4),
@@ -150,122 +155,159 @@ def tile_lstmmirrored_pb_kernel(tc, x, hist, ig, carousel, Wfx, Wfh, b_f, Wox, W
                 for kp in range(4):
                     mx_pass(step, r, kp)
 
+        def multiply_t(step):
+            grp, pair = step
+            for e in range(2):
+                acc[step, e] = psum.tile([P, 2, QW], F32, name="accT%d%d%d" % (grp, pair, e), tag="bank")
+                for j in range(2):
+                    cols = slice((2 * e + j) * P, (2 * e + j + 1) * P)
+                    for kp in range(4):
+                        s, g = divmod(kp, 2)
+                        a_codes, a_scales = a_q[s, pair]
+                        w_codes, w_scales = w_q[grp, kp]
+                        nc.tensor.matmul_mx(
+                            out=acc[step, e][:, j, :],
+                            lhsT=w_codes[:, cols].bitcast(E5M2X4),
+                            lhsT_scale=w_scales[:, cols],
+                            rhs=a_codes[:, g * QW : (g + 1) * QW].bitcast(E5M2X4),
+                            rhs_scale=a_scales[:, g * QW : (g + 1) * QW],
+                            start=(kp == 0),
+                            stop=(kp == 3),
+                        )
+
+        def gates_tile(step, shape):
+            gates[step] = stream.tile(shape, F32, name="gates%d%d" % step, tag="gates", bufs=4)
+
+        def sigmoid_t(step):
+            gates_tile(step, [P, 4, QW])
+            for blk in range(4):
+                col = 4 * step[0] + blk
+                nc.scalar.activation(out=gates[step][:, blk, :], in_=acc[step, blk // 2][:, blk % 2, :], func=SIGMOID, bias=bias_col[:, col : col + 1])
+
+        def turn_back(step):
+            for r in range(2):
+                back[step, r] = psum.tile([P, BANK], F32, name="back%d%d%d" % (*step, r), tag="bank")
+                for blk in range(4):
+                    nc.tensor.transpose(back[step, r][:, blk * P : (blk + 1) * P], gates[step][:, blk, r * P : (r + 1) * P], ident[:])
+
         def add_bias(step, r):
-            q = step[0]
+            gate, half = divmod(step[0], 2)
             if r == 0:
-                gates[step] = stream.tile([P, 2, 2, QW], F32, name="gates%d%d%d" % step, tag="gates", bufs=4)
-            nc.vector.tensor_tensor(
-                out=gates[step][:, r, :, :],
-                in0=acc[step, r][:].rearrange("p (e n) -> p e n", e=2),
-                in1=bias[:, :, q * QW : (q + 1) * QW],
-                op=ADD,
-            )
+                gates_tile(step, [P, 2, BANK])
+            nc.vector.tensor_tensor(out=gates[step][:, r, :], in0=acc[step, r][:], in1=bias[:, gate, half * BANK : (half + 1) * BANK], op=ADD)
 
-        def sigmoid(step):
-            flat = gates[step][:].rearrange("p r e n -> p (r e n)")
-            nc.scalar.activation(out=flat, in_=flat, func=SIGMOID)
+        def sigmoid(step, rows):
+            nc.scalar.activation(out=gates[step][:, rows, :], in_=gates[step][:, rows, :], func=SIGMOID)
 
-        def cell(step):
-            q, H, rp = step
-            if rp == 0:
-                c_out[q, H] = stream.tile([P, 4, QW], F32, name="c%d%d" % (q, H), tag="out", bufs=10)
-                h_out[q, H] = stream.tile([P, 4, QW], F32, name="h%d%d" % (q, H), tag="out", bufs=10)
-            c0 = (q % 2) * QW
-            nc.vector.scalar_tensor_tensor(
-                out=c_out[q, H][:, 2 * rp : 2 * rp + 2, :],
-                in0=gates[step][:, :, 0, :],
-                scalar=gain[:],
-                in1=ig_sb[H, q // 2][:, 2 * rp : 2 * rp + 2, c0 : c0 + QW],
-                op0=MULT,
-                op1=ADD,
-            )
+        def combine(step, rows):
+            grp, pair = step
+            gate, half = divmod(grp, 2)
+            cols = slice(half * BANK, (half + 1) * BANK)
+            value = back[step, rows.start][:].unsqueeze(1) if (step, 0) in back else gates[step][:, rows, :]
+            if gate == 0:
+                if pair not in c_out:
+                    c_out[pair] = keep.tile([P, 2, N], F32, name="c%d" % pair)
+                nc.vector.scalar_tensor_tensor(out=c_out[pair][:, rows, cols], in0=value, scalar=gain[:], in1=ig_sb[pair][:, rows, cols], op0=MULT, op1=ADD)
+            else:
+                if step not in h_out:
+                    h_out[step] = stream.tile([P, 2, BANK], F32, name="h%d%d" % step, tag="h", bufs=4)
+                nc.vector.tensor_tensor(out=h_out[step][:, rows, :], in0=value, in1=c_out[pair][:, rows, cols], op=MULT)
 
-        def hidden(step, engine):
-            q, H, rp = step
-            rows = slice(2 * rp, 2 * rp + 2)
-            engine.tensor_tensor(out=h_out[q, H][:, rows, :], in0=gates[step][:, :, 1, :], in1=c_out[q, H][:, rows, :], op=MULT)
+        def store(step, rows):
+            grp, pair = step
+            if grp == 1:
+                nc.sync.dma_start(out=pair_rows(out_1, pair), in_=c_out[pair][:])
+            elif grp >= 2:
+                cols = slice((grp - 2) * BANK, (grp - 1) * BANK)
+                nc.sync.dma_start(out=pair_rows(out_0, pair)[:, rows, cols], in_=h_out[step][:, rows, :])
 
-        def store(q, H, rows):
-            for dst, src in ((out_1, c_out), (out_0, h_out)):
-                nc.sync.dma_start(out=rows_view(dst)[H, :, rows, q * QW : (q + 1) * QW], in_=src[q, H][:, rows, :])
-
-
-        V, S = True, False
-        for item in [("w",0,0,2),("a",0,0),"c",("w",1,0,2),("a",1,0),("w",2,0,2),("a",0,1),("w",3,0,2),("a",1,1),("g",0,0),("a",0,2),("a",1,2),("w",0,2,2),("a",0,3),("a",1,3),("g",1,0),("w",1,2,2),("w",2,2,2),("w",3,2,2),("g",0,1),("g",1,1)]:
+        for item in [("w",0,0,2,(0,)),"c",("a",0,0),("w",0,0,2,(1,)),("a",1,0),("w",0,1),("a",0,1),("a",1,1),("w",0,2),("w",0,3),("g",0),("a",0,2),("a",1,2),("g",1),("w",1,0),("a",0,3),("a",1,3),("g",2),("w",1,1),("g",3),("w",1,2),("w",1,3)]:
             if item == "c":
                 load_consts()
             elif item[0] == "w":
                 load_w(*item[1:])
             elif item[0] == "a":
-                load_a(item[1], item[2] // 2, item[2] % 2)
+                load_a(*item[1:])
             else:
                 load_ig(*item[1:])
-        onv = [["VV","VV","VV","VS"],["SS","SS","SV","SV"],["VS","VS","SS","SS"],["SS","VS","SS","VS"]]
-        def prep_w(q, kp):
-            interleave_w(q, kp, 0, onv[q][kp][0] == "V")
-            interleave_w(q, kp, 1, onv[q][kp][1] == "V")
-            return (quantize_w, q, kp)
-        def prep_a(s, p):
-            transpose_a(s, p // 2, p % 2)
-            copy_a(s, p // 2, p % 2)
-            return (quantize_a, s, p // 2, p % 2)
-        pending = []
-        def prep(item):
-            new = prep_w(*item[1:]) if item[0] == "w" else prep_a(*item[1:])
-            flush()
-            pending.append(new)
-        def flush():
-            for f, *a in pending:
-                f(*a)
-            pending.clear()
-        steps = [(q, p // 2, p % 2) for q, p in [(0,0),(1,0),(0,1),(1,1),(0,2),(1,2),(0,3),(1,3),(2,0),(2,1),(2,2),(2,3),(3,0),(3,1),(3,2),(3,3)]]
+        onv = [0,0,["VS","VS","VS","VS"],["SS","VS","SS","VS"]]
+        steps = [(grp, pair) for pair in range(4) for grp in range(2)] + [(grp, pair) for grp in range(2, 4) for pair in range(4)]
         n_steps = len(steps)
-        done = set()
-        def early(step, kps):
-            flush()
+        CS = [2,5,8,11,14]
+        def passes(ks, kps):
             for kp in kps:
-                for r in range(2):
-                    mx_pass(step, r, kp)
-                    done.add((step, r, kp))
-        def mult(step):
-            flush()
-            for r in range(2):
-                for kp in range(4):
-                    if (step, r, kp) not in done:
-                        mx_pass(step, r, kp)
-        for item in [("w",0,0),("a",0,0),("w",1,0),"b",("w",0,1),("w",1,1),("e",0,[0,1]),("a",1,0),("e",1,[0,1]),("w",0,2),("a",0,1),("w",1,2),("e",0,[2]),("e",1,[2]),("w",0,3),("w",1,3)]:
-            if item == "b":
-                spread_bias()
-            elif item[0] == "e":
-                early(steps[item[1]], item[2])
-            else:
-                prep(item)
-        extras = {0:[("a",1,1)],1:[("a",0,2)],2:[("a",1,2),("w",2,0)],3:[("a",0,3)],4:[("a",1,3),("w",2,1)],5:[("w",2,2)],6:[("w",2,3)],7:[("w",3,0)],8:[("w",3,1)],9:[("w",3,2)],10:[("w",3,3)]}
-        AH = 1
-        for i in range(AH):
-            mult(steps[i])
-        stores = []
-        seen = set()
+                for k in ks:
+                    for r in range(2):
+                        mx_pass(steps[k], r, kp)
+        def mult(k):
+            if k in CS:
+                multiply_t(steps[k])
+            elif k >= 2:
+                multiply(steps[k])
+        V, S = True, False
+        F, O = 0, 1
+        both, first, second = slice(0, 2), slice(0, 1), slice(1, 2)
+
+        spread_bias()
+        turn_bias()
+        piece(0, 0, 0, V); piece(0, 0, 1, V)
+        turn_a(0, 0)
+        quantize_w(0, 0)
+        piece(1, 0, 0, V); piece(1, 0, 1, V); quant_a(0, 0); quantize_w(1, 0)
+        turn_a(1, 0)
+        passes([0, 1], [0])
+        piece(0, 1, 0, V); quant_a(1, 0); piece(0, 1, 1, V); piece(1, 1, 0, S); piece(1, 1, 1, V)
+        quantize_w(0, 1); quantize_w(1, 1)
+        turn_a(0, 1)
+        passes([0], [1])
+        turn_a(1, 1)
+        passes([1], [1])
+        quant_a(0, 1)
+        piece(0, 2, 0, V); piece(0, 2, 1, S); piece(1, 2, 0, V); piece(1, 2, 1, S); quantize_w(0, 2); quant_a(1, 1)
+        piece(0, 3, 0, V); piece(0, 3, 1, S); quantize_w(1, 2); piece(1, 3, 0, V); piece(1, 3, 1, S); quantize_w(0, 3)
+        passes([0, 1], [2]); passes([0], [3])
+        ready = [(quantize_w, 1, 3), (passes, [1], [3])]
+
+        extras = {0:[("a",0,2)],1:[("a",1,2)],2:[("a",0,3),("w",2,0)],3:[("a",1,3),("w",3,0)],4:[("w",2,1)],5:[("w",2,2)],6:[("w",2,3)],7:[("w",3,1)],8:[("w",3,2)],9:[("w",3,3)]}
         LAG = 2
         for i in range(n_steps + LAG):
-            pool = False
-            if i >= LAG:
-                cell(steps[i - LAG])
-                if pool:
-                    hidden(steps[i - LAG], nc.gpsimd)
-            if i < n_steps:
-                add_bias(steps[i], 0)
-                add_bias(steps[i], 1)
-                sigmoid(steps[i])
-            if i >= LAG:
-                if not pool:
-                    hidden(steps[i - LAG], nc.vector)
-                q, H, rp = steps[i - LAG]
-                if i - LAG >= n_steps - 4:
-                    store(q, H, slice(2 * rp, 2 * rp + 2))
-                elif rp == 1:
-                    store(q, H, slice(0, 4))
-            for item in extras.get(i, []):
-                prep(item)
-            if i + AH < n_steps:
-                mult(steps[i + AH])
+            k = i - LAG
+            todo = extras.get(i, [])
+            fill = []
+            if i < n_steps and i not in CS:
+                fill += [(add_bias, steps[i], 0), (add_bias, steps[i], 1)]
+            if k >= 0:
+                if k in CS or k == n_steps - 1:
+                    fill += [(combine, steps[k], first), (combine, steps[k], second)]
+                else:
+                    fill += [(combine, steps[k], both)]
+            fill += ready
+            ready = []
+            for item in todo:
+                if item[0] == "w":
+                    q, kp = item[1:]
+                    fill += [(piece, q, kp, part, V) for part in range(2) if onv[q][kp][part] == "V"]
+                    ready.append((quantize_w, q, kp))
+                else:
+                    ready.append((quant_a, *item[1:]))
+            if i in CS:
+                sigmoid_t(steps[i])
+            for f, *a in fill:
+                f(*a)
+            if i + 1 < n_steps:
+                mult(i + 1)
+            if i in CS:
+                turn_back(steps[i])
+            s_items = [(turn_a, *item[1:]) for item in todo if item[0] == "a"]
+            s_items += [(piece, *item[1:], part, S) for item in todo if item[0] == "w" for part in range(2) if onv[item[1]][item[2]][part] == "S"]
+            if i == n_steps - 1:
+                s_items = [(sigmoid, steps[i], first), (sigmoid, steps[i], second)]
+            elif i < n_steps and i not in CS:
+                s_items.insert(1, (sigmoid, steps[i], both))
+            for f, *a in s_items:
+                f(*a)
+            if k == n_steps - 1:
+                store(steps[k], first)
+                store(steps[k], second)
+            elif k >= 0:
+                store(steps[k], both)

@@ -18,17 +18,33 @@ SIGMOID = mybir.ActivationFunctionType.Sigmoid
 P = 128
 PACK = 4
 K_PASS = P * PACK
-QW = 256
-BANK = 512
+PASSES = 4
+GROUP = 512
+PART = 256
+PAIRS = 4
+PAIR_ROWS = 2 * P
+BLOCKS = GROUP // P
+RUN = 4
+
+STEPS = [(group, pair) for pair in range(PAIRS) for group in (0, 1)] + [(group, pair) for group in (2, 3) for pair in range(PAIRS)]
+LAST = len(STEPS) - 1
+OPENING = 3
+TURN_EVERY = 3
+TURNED = set(range(TURN_EVERY, LAST, TURN_EVERY)) | {LAST - 1}
+AHEAD = 2
+BEHIND = 2
 
 
 def tile_lstmmirrored_pb_kernel(tc, x, hist, ig, carousel, Wfx, Wfh, b_f, Wox, Woh, b_o, out_0, out_1):
     nc = tc.nc
-    acts = (x, hist)
+    sources = (x, hist)
     weights = ((Wfx, Wfh), (Wox, Woh))
 
-    def pair_rows(t, pair):
-        return t.rearrange("(m p r) n -> m p r n", m=4, r=2)[pair]
+    def pair_rows(tensor, pair):
+        return tensor.rearrange("(m p r) n -> m p r n", m=PAIRS, r=2)[pair]
+
+    def half_cols(half):
+        return slice(half * GROUP, (half + 1) * GROUP)
 
     with ExitStack() as ctx:
         keep = ctx.enter_context(tc.tile_pool(name="keep", bufs=1))
@@ -36,10 +52,25 @@ def tile_lstmmirrored_pb_kernel(tc, x, hist, ig, carousel, Wfx, Wfh, b_f, Wox, W
         psum = ctx.enter_context(tc.psum_pool(name="psum", bufs=8))
         ctx.enter_context(tc.manual_schedule(engines={mybir.EngineType.SP}))
 
+        def w_raw_tile(name):
+            return stream.tile([P, PACK, N], BF16, name=name, tag="w_raw", bufs=5)
+
+        def small_raw_tile(shape, name):
+            return stream.tile(shape, BF16, name=name, tag="small_raw", bufs=7)
+
+        def grouped_tile(name):
+            return stream.tile([P, PACK * GROUP], BF16, name=name, tag="grouped", bufs=5, align_bytes=64)
+
+        def gates_tile(shape, dtype, name):
+            return stream.tile(shape, dtype, name=name, tag="gates", bufs=4)
+
+        def bank_tile(shape, dtype, name):
+            return psum.tile(shape, dtype, name=name, tag="bank")
+
         ident = keep.tile([P, P], F32, name="ident")
         ones = keep.tile([P, P], BF16, name="ones")
-        bias_row = stream.tile([P, 2 * N], BF16, name="bias_row", tag="gates", bufs=4)
-        bias = keep.tile([P, 2, N], BF16, name="bias")
+        bias_row = gates_tile([P, 2 * N], BF16, "bias_row")
+        bias_wide = keep.tile([P, 2, N], BF16, name="bias_wide")
         bias_col = keep.tile([P, 2 * N // P], F32, name="bias_col")
         gain = keep.tile([P, 1], BF16, name="gain")
         make_identity(nc, ident[:])
@@ -47,267 +78,230 @@ def tile_lstmmirrored_pb_kernel(tc, x, hist, ig, carousel, Wfx, Wfh, b_f, Wox, W
         nc.vector.memset(ones[:], 1.0)
 
         w_raw, a_raw, ig_sb = {}, {}, {}
-        w_grouped, a_grouped, w_q, a_q = {}, {}, {}, {}
-        acc, gates, c_out, h_out, a_banks, back = {}, {}, {}, {}, {}, {}
+        w_grouped, a_grouped, w_mx, a_mx = {}, {}, {}, {}
+        sums, gates, turned_back, c_sb, h_sb = {}, {}, {}, {}, {}
 
-        def load_w(gate, kp, splits=1, halves=(0, 1)):
+        def w_rows(gate, kp):
             s, g = divmod(kp, 2)
-            src = weights[gate][s][g * K_PASS : (g + 1) * K_PASS, :].rearrange("(p j) n -> p j n", j=PACK)
-            if splits == 1:
-                t = stream.tile([P, PACK, N], BF16, name="w%d%d" % (gate, kp), tag="w_raw", bufs=5)
-                nc.sync.dma_start(out=t[:], in_=src)
-            for half in halves:
-                cols = slice(half * BANK, (half + 1) * BANK)
-                if splits == 2:
-                    t = stream.tile([P, PACK, BANK], BF16, name="w%d%d%d" % (gate, kp, half), tag="a_raw", bufs=7)
-                    nc.sync.dma_start(out=t[:], in_=src[:, :, cols])
-                    w_raw[2 * gate + half, kp] = t[:]
-                else:
-                    w_raw[2 * gate + half, kp] = t[:, :, cols]
+            return weights[gate][s][g * K_PASS : (g + 1) * K_PASS, :].rearrange("(p t) n -> p t n", t=PACK)
+
+        def load_w(gate, kp):
+            raw = w_raw_tile("w%d%d" % (gate, kp))
+            nc.sync.dma_start(out=raw[:], in_=w_rows(gate, kp))
+            for half in range(2):
+                w_raw[2 * gate + half, kp] = raw[:, :, half_cols(half)]
+
+        def load_first_w(half):
+            raw = small_raw_tile([P, PACK, GROUP], "w_first%d" % half)
+            nc.sync.dma_start(out=raw[:], in_=w_rows(0, 0)[:, :, half_cols(half)])
+            w_raw[half, 0] = raw[:]
 
         def load_a(s, pair):
-            t = stream.tile([P, 2, K], BF16, name="a%d%d" % (s, pair), tag="a_raw", bufs=7)
-            nc.sync.dma_start(out=t[:], in_=pair_rows(acts[s], pair))
-            a_raw[s, pair] = t
+            a_raw[s, pair] = small_raw_tile([P, 2, K], "a%d%d" % (s, pair))
+            nc.sync.dma_start(out=a_raw[s, pair][:], in_=pair_rows(sources[s], pair))
 
         def load_ig(pair):
-            t = keep.tile([P, 2, N], BF16, name="ig%d" % pair)
-            nc.sync.dma_start(out=t[:], in_=pair_rows(ig, pair))
-            ig_sb[pair] = t
+            ig_sb[pair] = keep.tile([P, 2, N], BF16, name="ig%d" % pair)
+            nc.sync.dma_start(out=ig_sb[pair][:], in_=pair_rows(ig, pair))
 
-        def load_consts():
+        def load_constants():
             for gate, b in enumerate((b_f, b_o)):
                 nc.sync.dma_start(out=bias_row[0:1, gate * N : (gate + 1) * N], in_=b.rearrange("(o n) -> o n", o=1))
             nc.sync.dma_start(out=gain[:], in_=carousel.partition_broadcast(P))
 
-        def spread_bias():
+        def spread_biases():
             for gate in range(2):
-                bank = psum.tile([P, N], BF16, name="bias_bank%d" % gate, tag="bank")
-                for c0 in range(0, N, BANK):
-                    nc.tensor.matmul(bank[:, c0 : c0 + BANK], ones[:], bias_row[:, gate * N + c0 : gate * N + c0 + BANK], start=True, stop=True)
-                nc.scalar.copy(out=bias[:, gate, :], in_=bank[:])
-
-        def turn_bias():
-            bank = psum.tile([P, 2 * N // P], F32, name="bias_col_bank", tag="bank")
-            for blk in range(2 * N // P):
-                nc.tensor.matmul(bank[:, blk : blk + 1], bias_row[:, blk * P : (blk + 1) * P], ones[:, 0:1], start=True, stop=True)
+                bank = bank_tile([P, N], BF16, "bias_wide_bank%d" % gate)
+                for half in range(2):
+                    rhs = bias_row[:, gate * N : (gate + 1) * N][:, half_cols(half)]
+                    nc.tensor.matmul(bank[:, half_cols(half)], ones[:], rhs, start=True, stop=True)
+                nc.scalar.copy(out=bias_wide[:, gate, :], in_=bank[:])
+            bank = bank_tile([P, 2 * N // P], F32, "bias_col_bank")
+            for j in range(2 * N // P):
+                nc.tensor.matmul(bank[:, j : j + 1], bias_row[:, j * P : (j + 1) * P], ones[:, 0:1], start=True, stop=True)
             nc.scalar.copy(out=bias_col[:], in_=bank[:])
 
-        def grouped_tile(name):
-            return stream.tile([P, PACK * BANK], BF16, name=name, tag="grouped", bufs=5, align_bytes=64)
+        def quantize(grouped, name):
+            codes = keep.tile([P, GROUP], U32, name=name + "_codes", align_bytes=64)
+            scales = keep.tile([P, GROUP], U8, name=name + "_scales", align_bytes=64)
+            nc.vector.quantize_mx(out=codes[:].bitcast(E5M2X4), scales=scales[:], in_=grouped[:])
+            return codes, scales
 
-        def piece(grp, kp, part, on_vector):
-            if (grp, kp) not in w_grouped:
-                w_grouped[grp, kp] = grouped_tile("wg%d%d" % (grp, kp))
-            dst = w_grouped[grp, kp][:, part * PACK * QW : (part + 1) * PACK * QW].rearrange("p (c i t) -> p c t i", i=4, t=PACK)
-            src = w_raw[grp, kp][:, :, part * QW : (part + 1) * QW].rearrange("p t (c i) -> p c t i", i=4)
+        def interleave_w(group, kp, part, on_vector):
+            if (group, kp) not in w_grouped:
+                w_grouped[group, kp] = grouped_tile("w_grouped%d%d" % (group, kp))
+            lo, hi = part * PART, (part + 1) * PART
+            dst = w_grouped[group, kp][:, PACK * lo : PACK * hi].rearrange("p (c i t) -> p c t i", i=RUN, t=PACK)
+            src = w_raw[group, kp][:, :, lo:hi].rearrange("p t (c i) -> p c t i", i=RUN)
             if on_vector:
                 nc.vector.tensor_copy(out=dst, in_=src)
             else:
                 nc.scalar.copy(out=dst, in_=src)
 
-        def quantize(grouped, name):
-            codes = keep.tile([P, BANK], U32, name=name + "_codes", align_bytes=64)
-            scales = keep.tile([P, BANK], U8, name=name + "_scales", align_bytes=64)
-            nc.vector.quantize_mx(out=codes[:].bitcast(E5M2X4), scales=scales[:], in_=grouped[:])
-            return codes, scales
-
-        def quantize_w(grp, kp):
-            w_q[grp, kp] = quantize(w_grouped[grp, kp], "wq%d%d" % (grp, kp))
+        def quantize_w(group, kp):
+            w_mx[group, kp] = quantize(w_grouped[group, kp], "w_mx%d%d" % (group, kp))
 
         def turn_a(s, pair):
             banks = []
             for r in range(2):
-                bank = psum.tile([P, 2, 2, P], F32, name="tr%d%d%d" % (s, pair, r), tag="bank")
+                bank = bank_tile([P, 2, 2, P], F32, "a_bank%d%d%d" % (s, pair, r))
                 words = a_raw[s, pair][:, r, :].bitcast(F32)
                 for g in range(2):
+                    g_words = words[:, g * K_PASS // 2 : (g + 1) * K_PASS // 2]
                     for u in range(2):
-                        nc.tensor.transpose(bank[:, g, u, :], words[:, 256 * g + u : 256 * (g + 1) : 2], ident[:])
+                        nc.tensor.transpose(bank[:, g, u, :], g_words[:, u::2], ident[:])
                 banks.append(bank)
-            a_grouped[s, pair] = grouped_tile("ag%d%d" % (s, pair))
+            a_grouped[s, pair] = grouped_tile("a_grouped%d%d" % (s, pair))
             dst = a_grouped[s, pair][:].bitcast(F32).rearrange("p (g r b u) -> p r g b u", g=2, r=2, u=2)
             for r in range(2):
                 nc.scalar.copy(out=dst[:, r, :, :, :], in_=banks[r][:].rearrange("p g u b -> p g b u"))
 
-        def quant_a(s, pair):
-            a_q[s, pair] = quantize(a_grouped[s, pair], "aq%d%d" % (s, pair))
+        def quantize_a(s, pair):
+            a_mx[s, pair] = quantize(a_grouped[s, pair], "a_mx%d%d" % (s, pair))
 
-        def mx_pass(step, r, kp):
-            grp, pair = step
-            s, g = divmod(kp, 2)
-            if kp == 0:
-                acc[step, r] = psum.tile([P, BANK], F32, name="acc%d%d%d" % (grp, pair, r), tag="bank")
-            a_codes, a_scales = a_q[s, pair]
-            w_codes, w_scales = w_q[grp, kp]
-            cols = slice((2 * g + r) * P, (2 * g + r + 1) * P)
+        def mx_pass(out, stationary, stationary_cols, moving, moving_cols, kp):
             nc.tensor.matmul_mx(
-                out=acc[step, r][:],
-                lhsT=a_codes[:, cols].bitcast(E5M2X4),
-                lhsT_scale=a_scales[:, cols],
-                rhs=w_codes[:].bitcast(E5M2X4),
-                rhs_scale=w_scales[:],
+                out=out,
+                lhsT=stationary[0][:, stationary_cols].bitcast(E5M2X4),
+                lhsT_scale=stationary[1][:, stationary_cols],
+                rhs=moving[0][:, moving_cols].bitcast(E5M2X4),
+                rhs_scale=moving[1][:, moving_cols],
                 start=(kp == 0),
-                stop=(kp == 3),
+                stop=(kp == PASSES - 1),
             )
 
-        def multiply(step):
-            for r in range(2):
-                for kp in range(4):
-                    mx_pass(step, r, kp)
+        def direct_pass(i, r, kp):
+            group, pair = STEPS[i]
+            s, g = divmod(kp, 2)
+            if kp == 0:
+                sums[i, r] = bank_tile([P, GROUP], F32, "sums%d_%d" % (i, r))
+            rows = slice(g * PAIR_ROWS + r * P, g * PAIR_ROWS + (r + 1) * P)
+            mx_pass(sums[i, r][:], a_mx[s, pair], rows, w_mx[group, kp], slice(0, GROUP), kp)
 
-        def multiply_t(step):
-            grp, pair = step
+        def multiply(i):
+            group, pair = STEPS[i]
+            if i not in TURNED:
+                for r in range(2):
+                    for kp in range(PASSES):
+                        direct_pass(i, r, kp)
+                return
             for e in range(2):
-                acc[step, e] = psum.tile([P, 2, QW], F32, name="accT%d%d%d" % (grp, pair, e), tag="bank")
+                sums[i, e] = bank_tile([P, 2, PAIR_ROWS], F32, "sums%d_%d" % (i, e))
                 for j in range(2):
                     cols = slice((2 * e + j) * P, (2 * e + j + 1) * P)
-                    for kp in range(4):
+                    for kp in range(PASSES):
                         s, g = divmod(kp, 2)
-                        a_codes, a_scales = a_q[s, pair]
-                        w_codes, w_scales = w_q[grp, kp]
-                        nc.tensor.matmul_mx(
-                            out=acc[step, e][:, j, :],
-                            lhsT=w_codes[:, cols].bitcast(E5M2X4),
-                            lhsT_scale=w_scales[:, cols],
-                            rhs=a_codes[:, g * QW : (g + 1) * QW].bitcast(E5M2X4),
-                            rhs_scale=a_scales[:, g * QW : (g + 1) * QW],
-                            start=(kp == 0),
-                            stop=(kp == 3),
-                        )
+                        rows = slice(g * PAIR_ROWS, (g + 1) * PAIR_ROWS)
+                        mx_pass(sums[i, e][:, j, :], w_mx[group, kp], cols, a_mx[s, pair], rows, kp)
 
-        def gates_tile(step, shape):
-            gates[step] = stream.tile(shape, F32, name="gates%d%d" % step, tag="gates", bufs=4)
+        def row_sets(i):
+            return (slice(0, 1), slice(1, 2)) if i in TURNED or i == LAST else (slice(0, 2),)
 
-        def sigmoid_t(step):
-            gates_tile(step, [P, 4, QW])
-            for blk in range(4):
-                col = 4 * step[0] + blk
-                nc.scalar.activation(out=gates[step][:, blk, :], in_=acc[step, blk // 2][:, blk % 2, :], func=SIGMOID, bias=bias_col[:, col : col + 1])
-
-        def turn_back(step):
+        def add_bias(i):
+            gate, half = divmod(STEPS[i][0], 2)
+            gates[i] = gates_tile([P, 2, GROUP], F32, "gates%d" % i)
             for r in range(2):
-                back[step, r] = psum.tile([P, BANK], F32, name="back%d%d%d" % (*step, r), tag="bank")
-                for blk in range(4):
-                    nc.tensor.transpose(back[step, r][:, blk * P : (blk + 1) * P], gates[step][:, blk, r * P : (r + 1) * P], ident[:])
+                nc.vector.tensor_tensor(out=gates[i][:, r, :], in0=sums[i, r][:], in1=bias_wide[:, gate, half_cols(half)], op=ADD)
 
-        def add_bias(step, r):
-            gate, half = divmod(step[0], 2)
-            if r == 0:
-                gates_tile(step, [P, 2, BANK])
-            nc.vector.tensor_tensor(out=gates[step][:, r, :], in0=acc[step, r][:], in1=bias[:, gate, half * BANK : (half + 1) * BANK], op=ADD)
+        def sigmoid_direct(i):
+            for rows in row_sets(i):
+                nc.scalar.activation(out=gates[i][:, rows, :], in_=gates[i][:, rows, :], func=SIGMOID)
 
-        def sigmoid(step, rows):
-            nc.scalar.activation(out=gates[step][:, rows, :], in_=gates[step][:, rows, :], func=SIGMOID)
+        def sigmoid_turned(i):
+            gates[i] = gates_tile([P, BLOCKS, PAIR_ROWS], F32, "gates%d" % i)
+            for block in range(BLOCKS):
+                j = BLOCKS * STEPS[i][0] + block
+                nc.scalar.activation(out=gates[i][:, block, :], in_=sums[i, block // 2][:, block % 2, :], func=SIGMOID, bias=bias_col[:, j : j + 1])
 
-        def combine(step, rows):
-            grp, pair = step
-            gate, half = divmod(grp, 2)
-            cols = slice(half * BANK, (half + 1) * BANK)
-            value = back[step, rows.start][:].unsqueeze(1) if (step, 0) in back else gates[step][:, rows, :]
-            if gate == 0:
-                if pair not in c_out:
-                    c_out[pair] = keep.tile([P, 2, N], F32, name="c%d" % pair)
-                nc.vector.scalar_tensor_tensor(out=c_out[pair][:, rows, cols], in0=value, scalar=gain[:], in1=ig_sb[pair][:, rows, cols], op0=MULT, op1=ADD)
-            else:
-                if step not in h_out:
-                    h_out[step] = stream.tile([P, 2, BANK], F32, name="h%d%d" % step, tag="h", bufs=4)
-                nc.vector.tensor_tensor(out=h_out[step][:, rows, :], in0=value, in1=c_out[pair][:, rows, cols], op=MULT)
+        def turn_back(i):
+            for r in range(2):
+                turned_back[i, r] = bank_tile([P, GROUP], F32, "back%d_%d" % (i, r))
+                for block in reversed(range(BLOCKS)):
+                    nc.tensor.transpose(turned_back[i, r][:, block * P : (block + 1) * P], gates[i][:, block, r * P : (r + 1) * P], ident[:])
 
-        def store(step, rows):
-            grp, pair = step
-            if grp == 1:
-                nc.sync.dma_start(out=pair_rows(out_1, pair), in_=c_out[pair][:])
-            elif grp >= 2:
-                cols = slice((grp - 2) * BANK, (grp - 1) * BANK)
-                nc.sync.dma_start(out=pair_rows(out_0, pair)[:, rows, cols], in_=h_out[step][:, rows, :])
-
-        for item in [("w",0,0,2,(0,)),"c",("a",0,0),("w",0,0,2,(1,)),("a",1,0),("w",0,1),("a",0,1),("a",1,1),("w",0,2),("w",0,3),("g",0),("a",0,2),("a",1,2),("g",1),("w",1,0),("a",0,3),("a",1,3),("g",2),("w",1,1),("g",3),("w",1,2),("w",1,3)]:
-            if item == "c":
-                load_consts()
-            elif item[0] == "w":
-                load_w(*item[1:])
-            elif item[0] == "a":
-                load_a(*item[1:])
-            else:
-                load_ig(*item[1:])
-        onv = [0,0,["VS","VS","VS","VS"],["SS","VS","SS","VS"]]
-        steps = [(grp, pair) for pair in range(4) for grp in range(2)] + [(grp, pair) for grp in range(2, 4) for pair in range(4)]
-        n_steps = len(steps)
-        CS = [2,5,8,11,14]
-        def passes(ks, kps):
-            for kp in kps:
-                for k in ks:
-                    for r in range(2):
-                        mx_pass(steps[k], r, kp)
-        def mult(k):
-            if k in CS:
-                multiply_t(steps[k])
-            elif k >= 2:
-                multiply(steps[k])
-        V, S = True, False
-        F, O = 0, 1
-        both, first, second = slice(0, 2), slice(0, 1), slice(1, 2)
-
-        spread_bias()
-        turn_bias()
-        piece(0, 0, 0, V); piece(0, 0, 1, V)
-        turn_a(0, 0)
-        quantize_w(0, 0)
-        piece(1, 0, 0, V); piece(1, 0, 1, V); quant_a(0, 0); quantize_w(1, 0)
-        turn_a(1, 0)
-        passes([0, 1], [0])
-        piece(0, 1, 0, V); quant_a(1, 0); piece(0, 1, 1, V); piece(1, 1, 0, S); piece(1, 1, 1, V)
-        quantize_w(0, 1); quantize_w(1, 1)
-        turn_a(0, 1)
-        passes([0], [1])
-        turn_a(1, 1)
-        passes([1], [1])
-        quant_a(0, 1)
-        piece(0, 2, 0, V); piece(0, 2, 1, S); piece(1, 2, 0, V); piece(1, 2, 1, S); quantize_w(0, 2); quant_a(1, 1)
-        piece(0, 3, 0, V); piece(0, 3, 1, S); quantize_w(1, 2); piece(1, 3, 0, V); piece(1, 3, 1, S); quantize_w(0, 3)
-        passes([0, 1], [2]); passes([0], [3])
-        ready = [(quantize_w, 1, 3), (passes, [1], [3])]
-
-        extras = {0:[("a",0,2)],1:[("a",1,2)],2:[("a",0,3),("w",2,0)],3:[("a",1,3),("w",3,0)],4:[("w",2,1)],5:[("w",2,2)],6:[("w",2,3)],7:[("w",3,1)],8:[("w",3,2)],9:[("w",3,3)]}
-        LAG = 2
-        for i in range(n_steps + LAG):
-            k = i - LAG
-            todo = extras.get(i, [])
-            fill = []
-            if i < n_steps and i not in CS:
-                fill += [(add_bias, steps[i], 0), (add_bias, steps[i], 1)]
-            if k >= 0:
-                if k in CS or k == n_steps - 1:
-                    fill += [(combine, steps[k], first), (combine, steps[k], second)]
+        def combine(i):
+            group, pair = STEPS[i]
+            gate, half = divmod(group, 2)
+            cols = half_cols(half)
+            if group == 0:
+                c_sb[pair] = keep.tile([P, 2, N], F32, name="c%d" % pair)
+            if gate == 1:
+                h_sb[i] = stream.tile([P, 2, GROUP], F32, name="h%d" % i, tag="h", bufs=4)
+            for rows in row_sets(i):
+                value = turned_back[i, rows.start][:].unsqueeze(1) if i in TURNED else gates[i][:, rows, :]
+                if gate == 0:
+                    nc.vector.scalar_tensor_tensor(out=c_sb[pair][:, rows, cols], in0=value, scalar=gain[:], in1=ig_sb[pair][:, rows, cols], op0=MULT, op1=ADD)
                 else:
-                    fill += [(combine, steps[k], both)]
-            fill += ready
-            ready = []
-            for item in todo:
-                if item[0] == "w":
-                    q, kp = item[1:]
-                    fill += [(piece, q, kp, part, V) for part in range(2) if onv[q][kp][part] == "V"]
-                    ready.append((quantize_w, q, kp))
-                else:
-                    ready.append((quant_a, *item[1:]))
-            if i in CS:
-                sigmoid_t(steps[i])
-            for f, *a in fill:
-                f(*a)
-            if i + 1 < n_steps:
-                mult(i + 1)
-            if i in CS:
-                turn_back(steps[i])
-            s_items = [(turn_a, *item[1:]) for item in todo if item[0] == "a"]
-            s_items += [(piece, *item[1:], part, S) for item in todo if item[0] == "w" for part in range(2) if onv[item[1]][item[2]][part] == "S"]
-            if i == n_steps - 1:
-                s_items = [(sigmoid, steps[i], first), (sigmoid, steps[i], second)]
-            elif i < n_steps and i not in CS:
-                s_items.insert(1, (sigmoid, steps[i], both))
-            for f, *a in s_items:
-                f(*a)
-            if k == n_steps - 1:
-                store(steps[k], first)
-                store(steps[k], second)
-            elif k >= 0:
-                store(steps[k], both)
+                    nc.vector.tensor_tensor(out=h_sb[i][:, rows, :], in0=value, in1=c_sb[pair][:, rows, cols], op=MULT)
+
+        def store(i):
+            group, pair = STEPS[i]
+            if group == 1:
+                nc.sync.dma_start(out=pair_rows(out_1, pair), in_=c_sb[pair][:])
+            elif group >= 2:
+                for rows in row_sets(i) if i == LAST else (slice(0, 2),):
+                    nc.sync.dma_start(out=pair_rows(out_0, pair)[:, rows, half_cols(group - 2)], in_=h_sb[i][:, rows, :])
+
+        load_first_w(0)
+        load_constants()
+        load_a(0, 0)
+        load_first_w(1)
+        load_a(1, 0)
+        load_w(0, 1)
+        load_a(0, 1)
+        load_a(1, 1)
+        load_w(0, 2)
+        load_w(0, 3)
+        for pair in (2, 3):
+            load_a(0, pair)
+            load_a(1, pair)
+            load_ig(pair - 2)
+            load_w(1, pair - 2)
+        for pair in (2, 3):
+            load_w(1, pair)
+            load_ig(pair)
+
+        spread_biases()
+        for kp in range(PASSES):
+            first_a = (kp % 2, kp // 2)
+            turn_a(*first_a)
+            for half in range(2):
+                interleave_w(half, kp, 0, on_vector=True)
+                interleave_w(half, kp, 1, on_vector=kp + half < 2)
+            quantize_w(0, kp)
+            quantize_a(*first_a)
+            quantize_w(1, kp)
+        for kp in range(PASSES):
+            for i in range(OPENING):
+                for r in range(2):
+                    direct_pass(i, r, kp)
+
+        late_a = [(s, pair) for pair in (2, 3) for s in range(2)]
+        late_w = [(group, kp) for group in (2, 3) for kp in range(PASSES)]
+        turn_a(*late_a[0])
+        for i in range(len(STEPS) + BEHIND):
+            w_now = late_w[i - 1] if 1 <= i <= len(late_w) else None
+            if i in TURNED:
+                sigmoid_turned(i)
+            elif i <= LAST:
+                add_bias(i)
+            if w_now:
+                interleave_w(*w_now, 1, on_vector=False)
+            if i <= LAST and i not in TURNED:
+                sigmoid_direct(i)
+            if 2 <= i <= len(late_w) + 1:
+                quantize_w(*late_w[i - 2])
+            if i >= BEHIND:
+                combine(i - BEHIND)
+            if i < len(late_a):
+                quantize_a(*late_a[i])
+            if i + 1 < len(late_a):
+                turn_a(*late_a[i + 1])
+            if i - 1 in TURNED:
+                turn_back(i - 1)
+            if OPENING <= i + AHEAD <= LAST:
+                multiply(i + AHEAD)
+            if w_now:
+                interleave_w(*w_now, 0, on_vector=w_now[0] == 2 or w_now[1] % 2 == 1)
+            if i >= BEHIND:
+                store(i - BEHIND)

@@ -28,9 +28,9 @@ RUN = 4
 
 STEPS = [(group, pair) for pair in range(PAIRS) for group in (0, 1)] + [(group, pair) for group in (2, 3) for pair in range(PAIRS)]
 LAST = len(STEPS) - 1
-OPENING = 3
-TURN_EVERY = 3
-TURNED = set(range(TURN_EVERY, LAST, TURN_EVERY)) | {LAST - 1}
+OPENING = 4
+TURNED = list(range(OPENING + 1, LAST, 2))
+TURNED_GROUPS = sorted({STEPS[i][0] for i in TURNED})
 AHEAD = 2
 BEHIND = 2
 
@@ -71,7 +71,7 @@ def tile_lstmmirrored_pb_kernel(tc, x, hist, ig, carousel, Wfx, Wfh, b_f, Wox, W
         ones = keep.tile([P, P], BF16, name="ones")
         bias_row = gates_tile([P, 2 * N], BF16, "bias_row")
         bias_wide = keep.tile([P, 2, N], BF16, name="bias_wide")
-        bias_col = keep.tile([P, 2 * N // P], F32, name="bias_col")
+        bias_col = keep.tile([P, len(TURNED_GROUPS), BLOCKS], F32, name="bias_col")
         gain = keep.tile([P, 1], BF16, name="gain")
         make_identity(nc, ident[:])
         nc.vector.memset(bias_row[:].bitcast(U32), 0)
@@ -116,9 +116,11 @@ def tile_lstmmirrored_pb_kernel(tc, x, hist, ig, carousel, Wfx, Wfh, b_f, Wox, W
                     rhs = bias_row[:, gate * N : (gate + 1) * N][:, half_cols(half)]
                     nc.tensor.matmul(bank[:, half_cols(half)], ones[:], rhs, start=True, stop=True)
                 nc.scalar.copy(out=bias_wide[:, gate, :], in_=bank[:])
-            bank = bank_tile([P, 2 * N // P], F32, "bias_col_bank")
-            for j in range(2 * N // P):
-                nc.tensor.matmul(bank[:, j : j + 1], bias_row[:, j * P : (j + 1) * P], ones[:, 0:1], start=True, stop=True)
+            bank = bank_tile([P, len(TURNED_GROUPS), BLOCKS], F32, "bias_col_bank")
+            for e, group in enumerate(TURNED_GROUPS):
+                for block in range(BLOCKS):
+                    first = group * GROUP + block * P
+                    nc.tensor.matmul(bank[:, e, block : block + 1], bias_row[:, first : first + P], ones[:, 0:1], start=True, stop=True)
             nc.scalar.copy(out=bias_col[:], in_=bank[:])
 
         def quantize(grouped, name):
@@ -170,20 +172,26 @@ def tile_lstmmirrored_pb_kernel(tc, x, hist, ig, carousel, Wfx, Wfh, b_f, Wox, W
                 stop=(kp == PASSES - 1),
             )
 
-        def direct_pass(i, r, kp):
+        def direct_banks(i):
+            if i == LAST:
+                return [(0, slice(0, GROUP)), (1, slice(0, PART)), (1, slice(PART, GROUP))]
+            return [(0, slice(0, GROUP)), (1, slice(0, GROUP))]
+
+        def direct_pass(i, e, kp):
             group, pair = STEPS[i]
             s, g = divmod(kp, 2)
+            r, cols = direct_banks(i)[e]
             if kp == 0:
-                sums[i, r] = bank_tile([P, GROUP], F32, "sums%d_%d" % (i, r))
+                sums[i, e] = bank_tile([P, cols.stop - cols.start], F32, "sums%d_%d" % (i, e))
             rows = slice(g * PAIR_ROWS + r * P, g * PAIR_ROWS + (r + 1) * P)
-            mx_pass(sums[i, r][:], a_mx[s, pair], rows, w_mx[group, kp], slice(0, GROUP), kp)
+            mx_pass(sums[i, e][:], a_mx[s, pair], rows, w_mx[group, kp], cols, kp)
 
         def multiply(i):
             group, pair = STEPS[i]
             if i not in TURNED:
-                for r in range(2):
+                for e in range(len(direct_banks(i))):
                     for kp in range(PASSES):
-                        direct_pass(i, r, kp)
+                        direct_pass(i, e, kp)
                 return
             for e in range(2):
                 sums[i, e] = bank_tile([P, 2, PAIR_ROWS], F32, "sums%d_%d" % (i, e))
@@ -194,24 +202,27 @@ def tile_lstmmirrored_pb_kernel(tc, x, hist, ig, carousel, Wfx, Wfh, b_f, Wox, W
                         rows = slice(g * PAIR_ROWS, (g + 1) * PAIR_ROWS)
                         mx_pass(sums[i, e][:, j, :], w_mx[group, kp], cols, a_mx[s, pair], rows, kp)
 
-        def row_sets(i):
-            return (slice(0, 1), slice(1, 2)) if i in TURNED or i == LAST else (slice(0, 2),)
+        def shares(i):
+            if i in TURNED or i == LAST:
+                return [(slice(r, r + 1), cols) for r, cols in direct_banks(i)]
+            return [(slice(0, 2), slice(0, GROUP))]
 
         def add_bias(i):
             gate, half = divmod(STEPS[i][0], 2)
             gates[i] = gates_tile([P, 2, GROUP], F32, "gates%d" % i)
-            for r in range(2):
-                nc.vector.tensor_tensor(out=gates[i][:, r, :], in0=sums[i, r][:], in1=bias_wide[:, gate, half_cols(half)], op=ADD)
+            bias = bias_wide[:, gate, half_cols(half)]
+            for e, (r, cols) in enumerate(direct_banks(i)):
+                nc.vector.tensor_tensor(out=gates[i][:, r, cols], in0=sums[i, e][:], in1=bias[:, cols], op=ADD)
 
         def sigmoid_direct(i):
-            for rows in row_sets(i):
-                nc.scalar.activation(out=gates[i][:, rows, :], in_=gates[i][:, rows, :], func=SIGMOID)
+            for rows, cols in shares(i):
+                nc.scalar.activation(out=gates[i][:, rows, cols], in_=gates[i][:, rows, cols], func=SIGMOID)
 
         def sigmoid_turned(i):
             gates[i] = gates_tile([P, BLOCKS, PAIR_ROWS], F32, "gates%d" % i)
+            bias = bias_col[:, TURNED_GROUPS.index(STEPS[i][0]), :]
             for block in range(BLOCKS):
-                j = BLOCKS * STEPS[i][0] + block
-                nc.scalar.activation(out=gates[i][:, block, :], in_=sums[i, block // 2][:, block % 2, :], func=SIGMOID, bias=bias_col[:, j : j + 1])
+                nc.scalar.activation(out=gates[i][:, block, :], in_=sums[i, block // 2][:, block % 2, :], func=SIGMOID, bias=bias[:, block : block + 1])
 
         def turn_back(i):
             for r in range(2):
@@ -222,25 +233,27 @@ def tile_lstmmirrored_pb_kernel(tc, x, hist, ig, carousel, Wfx, Wfh, b_f, Wox, W
         def combine(i):
             group, pair = STEPS[i]
             gate, half = divmod(group, 2)
-            cols = half_cols(half)
             if group == 0:
                 c_sb[pair] = keep.tile([P, 2, N], F32, name="c%d" % pair)
             if gate == 1:
                 h_sb[i] = stream.tile([P, 2, GROUP], F32, name="h%d" % i, tag="h", bufs=4)
-            for rows in row_sets(i):
-                value = turned_back[i, rows.start][:].unsqueeze(1) if i in TURNED else gates[i][:, rows, :]
+            c_half = c_sb[pair][:, :, half_cols(half)]
+            for rows, cols in shares(i):
+                value = turned_back[i, rows.start][:].unsqueeze(1) if i in TURNED else gates[i][:, rows, cols]
                 if gate == 0:
-                    nc.vector.scalar_tensor_tensor(out=c_sb[pair][:, rows, cols], in0=value, scalar=gain[:], in1=ig_sb[pair][:, rows, cols], op0=MULT, op1=ADD)
+                    ig_half = ig_sb[pair][:, :, half_cols(half)]
+                    nc.vector.scalar_tensor_tensor(out=c_half[:, rows, cols], in0=value, scalar=gain[:], in1=ig_half[:, rows, cols], op0=MULT, op1=ADD)
                 else:
-                    nc.vector.tensor_tensor(out=h_sb[i][:, rows, :], in0=value, in1=c_sb[pair][:, rows, cols], op=MULT)
+                    nc.vector.tensor_tensor(out=h_sb[i][:, rows, cols], in0=value, in1=c_half[:, rows, cols], op=MULT)
 
         def store(i):
             group, pair = STEPS[i]
             if group == 1:
                 nc.sync.dma_start(out=pair_rows(out_1, pair), in_=c_sb[pair][:])
             elif group >= 2:
-                for rows in row_sets(i) if i == LAST else (slice(0, 2),):
-                    nc.sync.dma_start(out=pair_rows(out_0, pair)[:, rows, half_cols(group - 2)], in_=h_sb[i][:, rows, :])
+                h_half = pair_rows(out_0, pair)[:, :, half_cols(group - 2)]
+                for rows, cols in shares(i) if i == LAST else [(slice(0, 2), slice(0, GROUP))]:
+                    nc.sync.dma_start(out=h_half[:, rows, cols], in_=h_sb[i][:, rows, cols])
 
         load_first_w(0)
         load_constants()
@@ -267,7 +280,7 @@ def tile_lstmmirrored_pb_kernel(tc, x, hist, ig, carousel, Wfx, Wfh, b_f, Wox, W
             turn_a(*first_a)
             for half in range(2):
                 interleave_w(half, kp, 0, on_vector=True)
-                interleave_w(half, kp, 1, on_vector=kp + half < 2)
+                interleave_w(half, kp, 1, on_vector=half == 0 and kp < 2)
             quantize_w(0, kp)
             quantize_a(*first_a)
             quantize_w(1, kp)
@@ -297,8 +310,9 @@ def tile_lstmmirrored_pb_kernel(tc, x, hist, ig, carousel, Wfx, Wfh, b_f, Wox, W
                 quantize_a(*late_a[i])
             if i + 1 < len(late_a):
                 turn_a(*late_a[i + 1])
-            if i - 1 in TURNED:
-                turn_back(i - 1)
+            for j in TURNED:
+                if i == (j + 1 if j <= len(late_w) + 1 else j):
+                    turn_back(j)
             if OPENING <= i + AHEAD <= LAST:
                 multiply(i + AHEAD)
             if w_now:

from contextlib import ExitStack

import concourse.mybir as mybir
from concourse.masks import make_identity

B, K, N = 1024, 1024, 1024
FLOPS = 4 * 2 * B * K * N

F32 = mybir.dt.float32
BF16 = mybir.dt.bfloat16
U32 = mybir.dt.uint32
U8 = mybir.dt.uint8
E5M2X4 = mybir.dt.float8_e5m2_x4
ADD = mybir.AluOpType.add
MULT = mybir.AluOpType.mult
SIGMOID = mybir.ActivationFunctionType.Sigmoid

P = 128
PACK = 4
K_PASS = P * PACK
PASSES = 4
GROUP = 512
PART = 256
PAIRS = 4
PAIR_ROWS = 2 * P
BLOCKS = GROUP // P
RUN = 4

STEPS = [(group, pair) for pair in range(PAIRS) for group in (0, 1)] + [(group, pair) for group in (2, 3) for pair in range(PAIRS)]
LAST = len(STEPS) - 1
OPENING = 4
TURNED = list(range(OPENING + 1, LAST, 2))
TURNED_GROUPS = sorted({STEPS[i][0] for i in TURNED})
AHEAD = 2
BEHIND = 2


def tile_lstmmirrored_pb_kernel(tc, x, hist, ig, carousel, Wfx, Wfh, b_f, Wox, Woh, b_o, out_0, out_1):
    nc = tc.nc
    sources = (x, hist)
    weights = ((Wfx, Wfh), (Wox, Woh))

    def pair_rows(tensor, pair):
        return tensor.rearrange("(m p r) n -> m p r n", m=PAIRS, r=2)[pair]

    def half_cols(half):
        return slice(half * GROUP, (half + 1) * GROUP)

    with ExitStack() as ctx:
        keep = ctx.enter_context(tc.tile_pool(name="keep", bufs=1))
        stream = ctx.enter_context(tc.tile_pool(name="stream", bufs=1))
        psum = ctx.enter_context(tc.psum_pool(name="psum", bufs=8))
        ctx.enter_context(tc.manual_schedule(engines={mybir.EngineType.SP}))

        def w_raw_tile(name):
            return stream.tile([P, PACK, N], BF16, name=name, tag="w_raw", bufs=5)

        def small_raw_tile(shape, name):
            return stream.tile(shape, BF16, name=name, tag="small_raw", bufs=7)

        def grouped_tile(name):
            return stream.tile([P, PACK * GROUP], BF16, name=name, tag="grouped", bufs=5, align_bytes=64)

        def gates_tile(shape, dtype, name):
            return stream.tile(shape, dtype, name=name, tag="gates", bufs=4)

        def bank_tile(shape, dtype, name):
            return psum.tile(shape, dtype, name=name, tag="bank")

        ident = keep.tile([P, P], F32, name="ident")
        ones = keep.tile([P, P], BF16, name="ones")
        bias_row = gates_tile([P, 2 * N], BF16, "bias_row")
        bias_wide = keep.tile([P, 2, N], BF16, name="bias_wide")
        bias_col = keep.tile([P, len(TURNED_GROUPS), BLOCKS], F32, name="bias_col")
        gain = keep.tile([P, 1], BF16, name="gain")
        make_identity(nc, ident[:])
        nc.vector.memset(bias_row[:].bitcast(U32), 0)
        nc.vector.memset(ones[:], 1.0)

        w_raw, a_raw, ig_sb = {}, {}, {}
        w_grouped, a_grouped, w_mx, a_mx = {}, {}, {}, {}
        sums, gates, turned_back, c_sb, h_sb = {}, {}, {}, {}, {}

        def w_rows(gate, kp):
            s, g = divmod(kp, 2)
            return weights[gate][s][g * K_PASS : (g + 1) * K_PASS, :].rearrange("(p t) n -> p t n", t=PACK)

        def load_w(gate, kp):
            raw = w_raw_tile("w%d%d" % (gate, kp))
            nc.sync.dma_start(out=raw[:], in_=w_rows(gate, kp))
            for half in range(2):
                w_raw[2 * gate + half, kp] = raw[:, :, half_cols(half)]

        def load_first_w(half):
            raw = small_raw_tile([P, PACK, GROUP], "w_first%d" % half)
            nc.sync.dma_start(out=raw[:], in_=w_rows(0, 0)[:, :, half_cols(half)])
            w_raw[half, 0] = raw[:]

        def load_a(s, pair):
            a_raw[s, pair] = small_raw_tile([P, 2, K], "a%d%d" % (s, pair))
            nc.sync.dma_start(out=a_raw[s, pair][:], in_=pair_rows(sources[s], pair))

        def load_ig(pair):
            ig_sb[pair] = keep.tile([P, 2, N], BF16, name="ig%d" % pair)
            nc.sync.dma_start(out=ig_sb[pair][:], in_=pair_rows(ig, pair))

        def load_constants():
            for gate, b in enumerate((b_f, b_o)):
                nc.sync.dma_start(out=bias_row[0:1, gate * N : (gate + 1) * N], in_=b.rearrange("(o n) -> o n", o=1))
            nc.sync.dma_start(out=gain[:], in_=carousel.partition_broadcast(P))

        def spread_biases():
            for gate in range(2):
                bank = bank_tile([P, N], BF16, "bias_wide_bank%d" % gate)
                for half in range(2):
                    rhs = bias_row[:, gate * N : (gate + 1) * N][:, half_cols(half)]
                    nc.tensor.matmul(bank[:, half_cols(half)], ones[:], rhs, start=True, stop=True)
                nc.scalar.copy(out=bias_wide[:, gate, :], in_=bank[:])
            bank = bank_tile([P, len(TURNED_GROUPS), BLOCKS], F32, "bias_col_bank")
            for e, group in enumerate(TURNED_GROUPS):
                for block in range(BLOCKS):
                    first = group * GROUP + block * P
                    nc.tensor.matmul(bank[:, e, block : block + 1], bias_row[:, first : first + P], ones[:, 0:1], start=True, stop=True)
            nc.scalar.copy(out=bias_col[:], in_=bank[:])

        def quantize(grouped, name):
            codes = keep.tile([P, GROUP], U32, name=name + "_codes", align_bytes=64)
            scales = keep.tile([P, GROUP], U8, name=name + "_scales", align_bytes=64)
            nc.vector.quantize_mx(out=codes[:].bitcast(E5M2X4), scales=scales[:], in_=grouped[:])
            return codes, scales

        def interleave_w(group, kp, part, on_vector):
            if (group, kp) not in w_grouped:
                w_grouped[group, kp] = grouped_tile("w_grouped%d%d" % (group, kp))
            lo, hi = part * PART, (part + 1) * PART
            dst = w_grouped[group, kp][:, PACK * lo : PACK * hi].rearrange("p (c i t) -> p c t i", i=RUN, t=PACK)
            src = w_raw[group, kp][:, :, lo:hi].rearrange("p t (c i) -> p c t i", i=RUN)
            if on_vector:
                nc.vector.tensor_copy(out=dst, in_=src)
            else:
                nc.scalar.copy(out=dst, in_=src)

        def quantize_w(group, kp):
            w_mx[group, kp] = quantize(w_grouped[group, kp], "w_mx%d%d" % (group, kp))

        def turn_a(s, pair):
            banks = []
            for r in range(2):
                bank = bank_tile([P, 2, 2, P], F32, "a_bank%d%d%d" % (s, pair, r))
                words = a_raw[s, pair][:, r, :].bitcast(F32)
                for g in range(2):
                    g_words = words[:, g * K_PASS // 2 : (g + 1) * K_PASS // 2]
                    for u in range(2):
                        nc.tensor.transpose(bank[:, g, u, :], g_words[:, u::2], ident[:])
                banks.append(bank)
            a_grouped[s, pair] = grouped_tile("a_grouped%d%d" % (s, pair))
            dst = a_grouped[s, pair][:].bitcast(F32).rearrange("p (g r b u) -> p r g b u", g=2, r=2, u=2)
            for r in range(2):
                nc.scalar.copy(out=dst[:, r, :, :, :], in_=banks[r][:].rearrange("p g u b -> p g b u"))

        def quantize_a(s, pair):
            a_mx[s, pair] = quantize(a_grouped[s, pair], "a_mx%d%d" % (s, pair))

        def mx_pass(out, stationary, stationary_cols, moving, moving_cols, kp):
            nc.tensor.matmul_mx(
                out=out,
                lhsT=stationary[0][:, stationary_cols].bitcast(E5M2X4),
                lhsT_scale=stationary[1][:, stationary_cols],
                rhs=moving[0][:, moving_cols].bitcast(E5M2X4),
                rhs_scale=moving[1][:, moving_cols],
                start=(kp == 0),
                stop=(kp == PASSES - 1),
            )

        def direct_banks(i):
            if i == LAST:
                return [(0, slice(0, GROUP)), (1, slice(0, PART)), (1, slice(PART, GROUP))]
            return [(0, slice(0, GROUP)), (1, slice(0, GROUP))]

        def direct_pass(i, e, kp):
            group, pair = STEPS[i]
            s, g = divmod(kp, 2)
            r, cols = direct_banks(i)[e]
            if kp == 0:
                sums[i, e] = bank_tile([P, cols.stop - cols.start], F32, "sums%d_%d" % (i, e))
            rows = slice(g * PAIR_ROWS + r * P, g * PAIR_ROWS + (r + 1) * P)
            mx_pass(sums[i, e][:], a_mx[s, pair], rows, w_mx[group, kp], cols, kp)

        def multiply(i):
            group, pair = STEPS[i]
            if i not in TURNED:
                for e in range(len(direct_banks(i))):
                    for kp in range(PASSES):
                        direct_pass(i, e, kp)
                return
            for e in range(2):
                sums[i, e] = bank_tile([P, 2, PAIR_ROWS], F32, "sums%d_%d" % (i, e))
                for j in range(2):
                    cols = slice((2 * e + j) * P, (2 * e + j + 1) * P)
                    for kp in range(PASSES):
                        s, g = divmod(kp, 2)
                        rows = slice(g * PAIR_ROWS, (g + 1) * PAIR_ROWS)
                        mx_pass(sums[i, e][:, j, :], w_mx[group, kp], cols, a_mx[s, pair], rows, kp)

        def shares(i):
            if i in TURNED or i == LAST:
                return [(slice(r, r + 1), cols) for r, cols in direct_banks(i)]
            return [(slice(0, 2), slice(0, GROUP))]

        def add_bias(i):
            gate, half = divmod(STEPS[i][0], 2)
            gates[i] = gates_tile([P, 2, GROUP], F32, "gates%d" % i)
            bias = bias_wide[:, gate, half_cols(half)]
            for e, (r, cols) in enumerate(direct_banks(i)):
                nc.vector.tensor_tensor(out=gates[i][:, r, cols], in0=sums[i, e][:], in1=bias[:, cols], op=ADD)

        def sigmoid_direct(i):
            for rows, cols in shares(i):
                nc.scalar.activation(out=gates[i][:, rows, cols], in_=gates[i][:, rows, cols], func=SIGMOID)

        def sigmoid_turned(i):
            gates[i] = gates_tile([P, BLOCKS, PAIR_ROWS], F32, "gates%d" % i)
            bias = bias_col[:, TURNED_GROUPS.index(STEPS[i][0]), :]
            for block in range(BLOCKS):
                nc.scalar.activation(out=gates[i][:, block, :], in_=sums[i, block // 2][:, block % 2, :], func=SIGMOID, bias=bias[:, block : block + 1])

        def turn_back(i):
            for r in range(2):
                turned_back[i, r] = bank_tile([P, GROUP], F32, "back%d_%d" % (i, r))
                for block in reversed(range(BLOCKS)):
                    nc.tensor.transpose(turned_back[i, r][:, block * P : (block + 1) * P], gates[i][:, block, r * P : (r + 1) * P], ident[:])

        def combine(i):
            group, pair = STEPS[i]
            gate, half = divmod(group, 2)
            if group == 0:
                c_sb[pair] = keep.tile([P, 2, N], F32, name="c%d" % pair)
            if gate == 1:
                h_sb[i] = stream.tile([P, 2, GROUP], F32, name="h%d" % i, tag="h", bufs=4)
            c_half = c_sb[pair][:, :, half_cols(half)]
            for rows, cols in shares(i):
                value = turned_back[i, rows.start][:].unsqueeze(1) if i in TURNED else gates[i][:, rows, cols]
                if gate == 0:
                    ig_half = ig_sb[pair][:, :, half_cols(half)]
                    nc.vector.scalar_tensor_tensor(out=c_half[:, rows, cols], in0=value, scalar=gain[:], in1=ig_half[:, rows, cols], op0=MULT, op1=ADD)
                else:
                    nc.vector.tensor_tensor(out=h_sb[i][:, rows, cols], in0=value, in1=c_half[:, rows, cols], op=MULT)

        def store(i):
            group, pair = STEPS[i]
            if group == 1:
                nc.sync.dma_start(out=pair_rows(out_1, pair), in_=c_sb[pair][:])
            elif group >= 2:
                h_half = pair_rows(out_0, pair)[:, :, half_cols(group - 2)]
                for rows, cols in shares(i) if i == LAST else [(slice(0, 2), slice(0, GROUP))]:
                    nc.sync.dma_start(out=h_half[:, rows, cols], in_=h_sb[i][:, rows, cols])

        load_first_w(0)
        load_constants()
        load_a(0, 0)
        load_first_w(1)
        load_a(1, 0)
        load_w(0, 1)
        load_a(0, 1)
        load_a(1, 1)
        load_w(0, 2)
        load_w(0, 3)
        for pair in (2, 3):
            load_a(0, pair)
            load_a(1, pair)
            load_ig(pair - 2)
            load_w(1, pair - 2)
        for pair in (2, 3):
            load_w(1, pair)
            load_ig(pair)

        spread_biases()
        for kp in range(PASSES):
            first_a = (kp % 2, kp // 2)
            turn_a(*first_a)
            for half in range(2):
                interleave_w(half, kp, 0, on_vector=True)
                interleave_w(half, kp, 1, on_vector=half == 0 and kp < 2)
            quantize_w(0, kp)
            quantize_a(*first_a)
            quantize_w(1, kp)
        for kp in range(PASSES):
            for i in range(OPENING):
                for r in range(2):
                    direct_pass(i, r, kp)

        late_a = [(s, pair) for pair in (2, 3) for s in range(2)]
        late_w = [(group, kp) for group in (2, 3) for kp in range(PASSES)]
        turn_a(*late_a[0])
        for i in range(len(STEPS) + BEHIND):
            w_now = late_w[i - 1] if 1 <= i <= len(late_w) else None
            if i in TURNED:
                sigmoid_turned(i)
            elif i <= LAST:
                add_bias(i)
            if w_now:
                interleave_w(*w_now, 1, on_vector=False)
            if i <= LAST and i not in TURNED:
                sigmoid_direct(i)
            if 2 <= i <= len(late_w) + 1:
                quantize_w(*late_w[i - 2])
            if i >= BEHIND:
                combine(i - BEHIND)
            if i < len(late_a):
                quantize_a(*late_a[i])
            if i + 1 < len(late_a):
                turn_a(*late_a[i + 1])
            for j in TURNED:
                if i == (j + 1 if j <= len(late_w) + 1 else j):
                    turn_back(j)
            if OPENING <= i + AHEAD <= LAST:
                multiply(i + AHEAD)
            if w_now:
                interleave_w(*w_now, 0, on_vector=w_now[0] == 2 or w_now[1] % 2 == 1)
            if i >= BEHIND:
                store(i - BEHIND)
